import numpy as np
import ml_dtypes

BF16 = ml_dtypes.bfloat16


def bf(x):
    return np.asarray(x, np.float32).astype(BF16)


def f32(x):
    return np.asarray(x, np.float32)


def f64(x):
    return np.asarray(x).astype(np.float64)


def striped(idx):
    return np.tile(idx.reshape(-1, 16).T, (8, 1))


O, D, S, N = 256, 128, 256, 128
ROT = 0.05


def setup_inputs():
    width = (0.6 + np.random.random((O, 1, 1))) / np.sqrt(2.0 * D)
    upper = np.triu(ROT * np.random.standard_normal((O, D, D)), 1)
    sym = upper + upper.transpose(0, 2, 1) + np.eye(D) * np.random.standard_normal((O, 1, D))
    amat = bf(np.ascontiguousarray((sym * width).transpose(2, 1, 0)))
    cen = f32(np.random.standard_normal((O, D)) * width[:, :, 0])
    x = bf(np.random.standard_normal((D, N)) * (0.5 + np.random.random((1, N))))
    b = f32(0.5 + np.random.random((O, 1)))
    base = f32(np.random.standard_normal((O, S)))
    return {"base": base, "x": x, "amat": amat, "cen": cen, "b": b, "offs": striped(np.random.permutation(S)[:N])}


def reference(base, x, amat, cen, b, offs):
    idx = offs[:16].T.reshape(-1)
    y = (f64(amat).reshape(D, D * O).T @ f64(x)).reshape(D, O, N) + f64(cen).T[:, :, None]
    r2 = np.sum(y * y, axis=0)
    res = f64(base).copy()
    res[:, idx] = np.log(r2) * f64(b)
    return res

@@ -1,0 +1,90 @@
+import concourse.mybir as mybir
+
+F32 = mybir.dt.float32
+BF16 = mybir.dt.bfloat16
+U16 = mybir.dt.uint16
+ADD = mybir.AluOpType.add
+MULT = mybir.AluOpType.mult
+SQUARE = mybir.ActivationFunctionType.Square
+LN = mybir.ActivationFunctionType.Ln
+
+P = 128
+O, D, S, N = 256, 128, 256, 128
+BLOCKS = O // P
+LOAD = 8
+GROUP = 4
+
+FLOPS = 2 * D * D * O * N
+
+
+def tile_fuzzybelllayer_kernel(tc, base, x, amat, cen, b, offs, out):
+    nc = tc.nc
+    with (
+        tc.tile_pool(name="held", bufs=1) as held,
+        tc.tile_pool(name="squares", bufs=4) as squares,
+        tc.psum_pool(name="spread", bufs=1) as spread,
+        tc.psum_pool(name="products", bufs=7) as products,
+    ):
+        offsets = held.tile([P, N // 16], U16, name="offsets")
+        nc.sync.dma_start(offsets[:], offs)
+        x_sb = held.tile([P, N], BF16, name="x_sb")
+        nc.sync.dma_start(x_sb[:], x)
+        cen_sb = [held.tile([P, D], F32, name=f"cen{r}") for r in range(BLOCKS)]
+        for r in range(BLOCKS):
+            nc.sync.dma_start(cen_sb[r][:], cen[r * P : (r + 1) * P, :])
+
+        amat_sb = [held.tile([P, LOAD, O], BF16, name=f"amat{c}") for c in range(D // LOAD)]
+        for c in range(D // LOAD):
+            nc.sync.dma_start(amat_sb[c][:], amat[:, c * LOAD : (c + 1) * LOAD, :])
+
+        window = [held.tile([P, S], F32, name=f"window{r}") for r in range(BLOCKS)]
+        for r in range(BLOCKS):
+            nc.gpsimd.dma_start(window[r][:], base[r * P : (r + 1) * P, :])
+
+        b_row = held.tile([1, O], F32, name="b_row")
+        nc.gpsimd.dma_start(b_row[:], b.rearrange("o one -> one o"))
+        ones_row = held.tile([1, N], F32, name="ones_row")
+        nc.vector.memset(ones_row[:], 1.0)
+        b_ps = spread.tile([P, BLOCKS * N], F32, name="b_ps")
+        for r in range(BLOCKS):
+            nc.tensor.matmul(
+                b_ps[:, r * N : (r + 1) * N],
+                b_row[:, r * P : (r + 1) * P],
+                ones_row[:],
+                start=True,
+                stop=True,
+            )
+        b_wide = held.tile([P, BLOCKS * N], F32, name="b_wide")
+        nc.vector.tensor_copy(b_wide[:], b_ps[:])
+
+        for r in range(BLOCKS):
+            total = held.tile([P, GROUP * N], F32, name=f"total{r}")
+            for g in range(D // GROUP):
+                sq = total if g == 0 else squares.tile([P, GROUP * N], F32, name="sq")
+                for q in range(GROUP):
+                    i = g * GROUP + q
+                    z = products.tile([P, N], F32, name="z")
+                    nc.tensor.matmul(
+                        z[:],
+                        amat_sb[i // LOAD][:, i % LOAD, r * P : (r + 1) * P],
+                        x_sb[:],
+                        start=True,
+                        stop=True,
+                    )
+                    nc.scalar.activation(
+                        sq[:, q * N : (q + 1) * N], z[:], SQUARE, bias=cen_sb[r][:, i : i + 1]
+                    )
+                if g > 0:
+                    nc.vector.tensor_tensor(total[:], total[:], sq[:], ADD)
+
+            half = held.tile([P, 2 * N], F32, name=f"half{r}")
+            nc.vector.tensor_tensor(half[:], total[:, : 2 * N], total[:, 2 * N :], ADD)
+            r2 = held.tile([P, N], F32, name=f"r2_{r}")
+            nc.vector.tensor_tensor(r2[:], half[:, :N], half[:, N:], ADD)
+            log_r2 = held.tile([P, N], F32, name=f"log_r2_{r}")
+            nc.scalar.activation(log_r2[:], r2[:], LN)
+
+            nc.vector.tensor_tensor(
+                window[r][:].indirect(offsets[:]), log_r2[:], b_wide[:, r * N : (r + 1) * N], MULT
+            )
+            nc.sync.dma_start(out[r * P : (r + 1) * P, :], window[r][:])

@@ -13,6 +13,7 @@ O, D, S, N = 256, 128, 256, 128
 BLOCKS = O // P
 LOAD = 8
 GROUP = 4
+LANES = 2
 
 FLOPS = 2 * D * D * O * N
 
@@ -29,6 +30,8 @@ def tile_fuzzybelllayer_kernel(tc, base, x, amat, cen, b, offs, out):
         nc.sync.dma_start(offsets[:], offs)
         x_sb = held.tile([P, N], BF16, name="x_sb")
         nc.sync.dma_start(x_sb[:], x)
+        b_row = held.tile([1, O], F32, name="b_row")
+        nc.sync.dma_start(b_row[:], b.rearrange("o one -> one o"))
         cen_sb = [held.tile([P, D], F32, name=f"cen{r}") for r in range(BLOCKS)]
         for r in range(BLOCKS):
             nc.sync.dma_start(cen_sb[r][:], cen[r * P : (r + 1) * P, :])
@@ -39,10 +42,8 @@ def tile_fuzzybelllayer_kernel(tc, base, x, amat, cen, b, offs, out):
 
         window = [held.tile([P, S], F32, name=f"window{r}") for r in range(BLOCKS)]
         for r in range(BLOCKS):
-            nc.gpsimd.dma_start(window[r][:], base[r * P : (r + 1) * P, :])
+            nc.scalar.dma_start(window[r][:], base[r * P : (r + 1) * P, :])
 
-        b_row = held.tile([1, O], F32, name="b_row")
-        nc.gpsimd.dma_start(b_row[:], b.rearrange("o one -> one o"))
         ones_row = held.tile([1, N], F32, name="ones_row")
         nc.vector.memset(ones_row[:], 1.0)
         b_ps = spread.tile([P, BLOCKS * N], F32, name="b_ps")
@@ -58,29 +59,35 @@ def tile_fuzzybelllayer_kernel(tc, base, x, amat, cen, b, offs, out):
         nc.vector.tensor_copy(b_wide[:], b_ps[:])
 
         for r in range(BLOCKS):
-            total = held.tile([P, GROUP * N], F32, name=f"total{r}")
+            total = held.tile([P, LANES, GROUP * N], F32, name=f"total{r}")
             for g in range(D // GROUP):
-                sq = total if g == 0 else squares.tile([P, GROUP * N], F32, name="sq")
+                lane = total[:, g % LANES, :]
+                sq = lane if g < LANES else squares.tile([P, GROUP * N], F32, name="sq")[:]
+                z = products.tile([P, GROUP * N], F32, name="z")
                 for q in range(GROUP):
                     i = g * GROUP + q
-                    z = products.tile([P, N], F32, name="z")
                     nc.tensor.matmul(
-                        z[:],
+                        z[:, q * N : (q + 1) * N],
                         amat_sb[i // LOAD][:, i % LOAD, r * P : (r + 1) * P],
                         x_sb[:],
                         start=True,
                         stop=True,
                     )
+                for q in range(GROUP):
+                    i = g * GROUP + q
                     nc.scalar.activation(
-                        sq[:, q * N : (q + 1) * N], z[:], SQUARE, bias=cen_sb[r][:, i : i + 1]
+                        sq[:, q * N : (q + 1) * N],
+                        z[:, q * N : (q + 1) * N],
+                        SQUARE,
+                        bias=cen_sb[r][:, i : i + 1],
                     )
-                if g > 0:
-                    nc.vector.tensor_tensor(total[:], total[:], sq[:], ADD)
+                if g >= LANES:
+                    nc.vector.tensor_tensor(lane, lane, sq, ADD)
 
-            half = held.tile([P, 2 * N], F32, name=f"half{r}")
-            nc.vector.tensor_tensor(half[:], total[:, : 2 * N], total[:, 2 * N :], ADD)
             r2 = held.tile([P, N], F32, name=f"r2_{r}")
-            nc.vector.tensor_tensor(r2[:], half[:, :N], half[:, N:], ADD)
+            nc.vector.tensor_reduce(
+                r2[:], total[:].rearrange("o l (q j) -> o j (l q)", j=N), mybir.AxisListType.X, ADD
+            )
             log_r2 = held.tile([P, N], F32, name=f"log_r2_{r}")
             nc.scalar.activation(log_r2[:], r2[:], LN)
 

@@ -1,9 +1,11 @@
 import concourse.mybir as mybir
+from concourse.masks import make_identity
 
 F32 = mybir.dt.float32
 BF16 = mybir.dt.bfloat16
 U16 = mybir.dt.uint16
 ADD = mybir.AluOpType.add
+SUBTRACT = mybir.AluOpType.subtract
 MULT = mybir.AluOpType.mult
 SQUARE = mybir.ActivationFunctionType.Square
 LN = mybir.ActivationFunctionType.Ln
@@ -14,6 +16,9 @@ BLOCKS = O // P
 LOAD = 8
 GROUP = 4
 LANES = 2
+SLOTS = 4
+FEATS = P // SLOTS
+SETS = D // FEATS
 
 FLOPS = 2 * D * D * O * N
 
@@ -23,18 +28,17 @@ def tile_fuzzybelllayer_kernel(tc, base, x, amat, cen, b, offs, out):
     with (
         tc.tile_pool(name="held", bufs=1) as held,
         tc.tile_pool(name="squares", bufs=4) as squares,
-        tc.psum_pool(name="spread", bufs=1) as spread,
-        tc.psum_pool(name="products", bufs=7) as products,
+        tc.psum_pool(name="small", bufs=1) as small,
+        tc.psum_pool(name="banks", bufs=6) as banks,
     ):
         offsets = held.tile([P, N // 16], U16, name="offsets")
         nc.sync.dma_start(offsets[:], offs)
+        cen_sb = held.tile([P, BLOCKS, D], F32, name="cen_sb")
+        nc.sync.dma_start(cen_sb[:], cen.rearrange("(r o) i -> o r i", o=P))
         x_sb = held.tile([P, N], BF16, name="x_sb")
         nc.sync.dma_start(x_sb[:], x)
         b_row = held.tile([1, O], F32, name="b_row")
         nc.sync.dma_start(b_row[:], b.rearrange("o one -> one o"))
-        cen_sb = [held.tile([P, D], F32, name=f"cen{r}") for r in range(BLOCKS)]
-        for r in range(BLOCKS):
-            nc.sync.dma_start(cen_sb[r][:], cen[r * P : (r + 1) * P, :])
 
         amat_sb = [held.tile([P, LOAD, O], BF16, name=f"amat{c}") for c in range(D // LOAD)]
         for c in range(D // LOAD):
@@ -44,9 +48,34 @@ def tile_fuzzybelllayer_kernel(tc, base, x, amat, cen, b, offs, out):
         for r in range(BLOCKS):
             nc.scalar.dma_start(window[r][:], base[r * P : (r + 1) * P, :])
 
+        split = held.tile([P, BLOCKS * SETS, SLOTS, FEATS], BF16, name="split")
+        whole = cen_sb[:].rearrange("o r (s f) -> o (r s) f", f=FEATS)
+        high, middle, low, zeros = (split[:, :, slot, :] for slot in range(SLOTS))
+        rest = held.tile([P, BLOCKS * SETS, FEATS], F32, name="rest")
+        nc.vector.tensor_copy(high, whole)
+        nc.vector.tensor_tensor(middle, whole, high, SUBTRACT)
+        nc.vector.tensor_tensor(rest[:], whole, high, SUBTRACT)
+        nc.vector.tensor_tensor(low, rest[:], middle, SUBTRACT)
+        nc.vector.memset(zeros, 0.0)
+        ident = held.tile([P, P], BF16, name="ident")
+        make_identity(nc, ident[:])
+        cen_rows = held.tile([P, SETS, O], BF16, name="cen_rows")
+        for s in range(SETS):
+            turned = small.tile([P, O], BF16, name="turned")
+            for r in range(BLOCKS):
+                nc.tensor.transpose(
+                    turned[:, r * P : (r + 1) * P],
+                    split[:, r * SETS + s, :, :].rearrange("o piece f -> o (piece f)"),
+                    ident[:],
+                )
+            nc.vector.tensor_copy(cen_rows[:, s, :], turned[:])
+        pick_col = held.tile([P, FEATS], BF16, name="pick_col")
+        nc.vector.tensor_tensor(pick_col[:], ident[:, :FEATS], ident[:, FEATS : 2 * FEATS], ADD)
+        nc.vector.tensor_tensor(pick_col[:], pick_col[:], ident[:, 2 * FEATS : 3 * FEATS], ADD)
+
         ones_row = held.tile([1, N], F32, name="ones_row")
         nc.vector.memset(ones_row[:], 1.0)
-        b_ps = spread.tile([P, BLOCKS * N], F32, name="b_ps")
+        b_ps = small.tile([P, BLOCKS * N], F32, name="b_ps")
         for r in range(BLOCKS):
             nc.tensor.matmul(
                 b_ps[:, r * N : (r + 1) * N],
@@ -61,26 +90,28 @@ def tile_fuzzybelllayer_kernel(tc, base, x, amat, cen, b, offs, out):
         for r in range(BLOCKS):
             total = held.tile([P, LANES, GROUP * N], F32, name=f"total{r}")
             for g in range(D // GROUP):
-                lane = total[:, g % LANES, :]
-                sq = lane if g < LANES else squares.tile([P, GROUP * N], F32, name="sq")[:]
-                z = products.tile([P, GROUP * N], F32, name="z")
+                first = g * GROUP
+                y = banks.tile([P, GROUP, N], F32, name="y")
                 for q in range(GROUP):
-                    i = g * GROUP + q
+                    i = first + q
                     nc.tensor.matmul(
-                        z[:, q * N : (q + 1) * N],
+                        y[:, q, :],
                         amat_sb[i // LOAD][:, i % LOAD, r * P : (r + 1) * P],
                         x_sb[:],
-                        start=True,
-                        stop=True,
+                        start=(q == 0),
+                        stop=False,
                     )
-                for q in range(GROUP):
-                    i = g * GROUP + q
-                    nc.scalar.activation(
-                        sq[:, q * N : (q + 1) * N],
-                        z[:, q * N : (q + 1) * N],
-                        SQUARE,
-                        bias=cen_sb[r][:, i : i + 1],
-                    )
+                picked = pick_col[:, first % FEATS : first % FEATS + GROUP]
+                nc.tensor.matmul(
+                    y[:],
+                    cen_rows[:, first // FEATS, r * P : (r + 1) * P],
+                    picked.unsqueeze(2).to_broadcast([P, GROUP, N]),
+                    start=False,
+                    stop=True,
+                )
+                lane = total[:, g % LANES, :]
+                sq = lane if g < LANES else squares.tile([P, GROUP * N], F32, name="sq")[:]
+                nc.scalar.activation(sq, y[:].rearrange("o q j -> o (q j)"), SQUARE)
                 if g >= LANES:
                     nc.vector.tensor_tensor(lane, lane, sq, ADD)
 

@@ -15,7 +15,9 @@ O, D, S, N = 256, 128, 256, 128
 BLOCKS = O // P
 LOAD = 8
 GROUP = 4
+GROUPS = D // GROUP
 LANES = 2
+LAG = 4
 SLOTS = 4
 FEATS = P // SLOTS
 SETS = D // FEATS
@@ -75,6 +77,8 @@ def tile_fuzzybelllayer_kernel(tc, base, x, amat, cen, b, offs, out):
 
         ones_row = held.tile([1, N], F32, name="ones_row")
         nc.vector.memset(ones_row[:], 1.0)
+        warm = held.tile([1, N], F32, name="warm")
+        nc.scalar.activation(warm[:], ones_row[:], LN)
         b_ps = small.tile([P, BLOCKS * N], F32, name="b_ps")
         for r in range(BLOCKS):
             nc.tensor.matmul(
@@ -87,9 +91,12 @@ def tile_fuzzybelllayer_kernel(tc, base, x, amat, cen, b, offs, out):
         b_wide = held.tile([P, BLOCKS * N], F32, name="b_wide")
         nc.vector.tensor_copy(b_wide[:], b_ps[:])
 
-        for r in range(BLOCKS):
-            total = held.tile([P, LANES, GROUP * N], F32, name=f"total{r}")
-            for g in range(D // GROUP):
+        total = [held.tile([P, LANES, GROUP * N], F32, name=f"total{r}") for r in range(BLOCKS)]
+        for step in range(GROUPS + LAG * (BLOCKS - 1)):
+            for r in range(BLOCKS):
+                g = step - LAG * r
+                if g < 0 or g >= GROUPS:
+                    continue
                 first = g * GROUP
                 y = banks.tile([P, GROUP, N], F32, name="y")
                 for q in range(GROUP):
@@ -109,20 +116,21 @@ def tile_fuzzybelllayer_kernel(tc, base, x, amat, cen, b, offs, out):
                     start=False,
                     stop=True,
                 )
-                lane = total[:, g % LANES, :]
+                lane = total[r][:, g % LANES, :]
                 sq = lane if g < LANES else squares.tile([P, GROUP * N], F32, name="sq")[:]
                 nc.scalar.activation(sq, y[:].rearrange("o q j -> o (q j)"), SQUARE)
                 if g >= LANES:
                     nc.vector.tensor_tensor(lane, lane, sq, ADD)
+                if g < GROUPS - 1:
+                    continue
 
-            r2 = held.tile([P, N], F32, name=f"r2_{r}")
-            nc.vector.tensor_reduce(
-                r2[:], total[:].rearrange("o l (q j) -> o j (l q)", j=N), mybir.AxisListType.X, ADD
-            )
-            log_r2 = held.tile([P, N], F32, name=f"log_r2_{r}")
-            nc.scalar.activation(log_r2[:], r2[:], LN)
-
-            nc.vector.tensor_tensor(
-                window[r][:].indirect(offsets[:]), log_r2[:], b_wide[:, r * N : (r + 1) * N], MULT
-            )
-            nc.sync.dma_start(out[r * P : (r + 1) * P, :], window[r][:])
+                r2 = held.tile([P, N], F32, name=f"r2_{r}")
+                nc.vector.tensor_reduce(
+                    r2[:], total[r][:].rearrange("o l (q j) -> o j (l q)", j=N), mybir.AxisListType.X, ADD
+                )
+                log_r2 = held.tile([P, N], F32, name=f"log_r2_{r}")
+                nc.scalar.activation(log_r2[:], r2[:], LN)
+                nc.vector.tensor_tensor(
+                    window[r][:].indirect(offsets[:]), log_r2[:], b_wide[:, r * N : (r + 1) * N], MULT
+                )
+                nc.sync.dma_start(out[r * P : (r + 1) * P, :], window[r][:])

@@ -1,11 +1,9 @@
 import concourse.mybir as mybir
-from concourse.masks import make_identity
 
 F32 = mybir.dt.float32
 BF16 = mybir.dt.bfloat16
 U16 = mybir.dt.uint16
 ADD = mybir.AluOpType.add
-SUBTRACT = mybir.AluOpType.subtract
 MULT = mybir.AluOpType.mult
 SQUARE = mybir.ActivationFunctionType.Square
 LN = mybir.ActivationFunctionType.Ln
@@ -15,12 +13,8 @@ O, D, S, N = 256, 128, 256, 128
 BLOCKS = O // P
 LOAD = 8
 GROUP = 4
-GROUPS = D // GROUP
 LANES = 2
-LAG = 4
-SLOTS = 4
-FEATS = P // SLOTS
-SETS = D // FEATS
+RELIEF = 16
 
 FLOPS = 2 * D * D * O * N
 
@@ -30,17 +24,18 @@ def tile_fuzzybelllayer_kernel(tc, base, x, amat, cen, b, offs, out):
     with (
         tc.tile_pool(name="held", bufs=1) as held,
         tc.tile_pool(name="squares", bufs=4) as squares,
-        tc.psum_pool(name="small", bufs=1) as small,
-        tc.psum_pool(name="banks", bufs=6) as banks,
+        tc.psum_pool(name="spread", bufs=1) as spread,
+        tc.psum_pool(name="products", bufs=7) as products,
     ):
         offsets = held.tile([P, N // 16], U16, name="offsets")
         nc.sync.dma_start(offsets[:], offs)
-        cen_sb = held.tile([P, BLOCKS, D], F32, name="cen_sb")
-        nc.sync.dma_start(cen_sb[:], cen.rearrange("(r o) i -> o r i", o=P))
         x_sb = held.tile([P, N], BF16, name="x_sb")
         nc.sync.dma_start(x_sb[:], x)
         b_row = held.tile([1, O], F32, name="b_row")
         nc.sync.dma_start(b_row[:], b.rearrange("o one -> one o"))
+        cen_sb = [held.tile([P, D], F32, name=f"cen{r}") for r in range(BLOCKS)]
+        for r in range(BLOCKS):
+            nc.sync.dma_start(cen_sb[r][:], cen[r * P : (r + 1) * P, :])
 
         amat_sb = [held.tile([P, LOAD, O], BF16, name=f"amat{c}") for c in range(D // LOAD)]
         for c in range(D // LOAD):
@@ -50,36 +45,11 @@ def tile_fuzzybelllayer_kernel(tc, base, x, amat, cen, b, offs, out):
         for r in range(BLOCKS):
             nc.scalar.dma_start(window[r][:], base[r * P : (r + 1) * P, :])
 
-        split = held.tile([P, BLOCKS * SETS, SLOTS, FEATS], BF16, name="split")
-        whole = cen_sb[:].rearrange("o r (s f) -> o (r s) f", f=FEATS)
-        high, middle, low, zeros = (split[:, :, slot, :] for slot in range(SLOTS))
-        rest = held.tile([P, BLOCKS * SETS, FEATS], F32, name="rest")
-        nc.vector.tensor_copy(high, whole)
-        nc.vector.tensor_tensor(middle, whole, high, SUBTRACT)
-        nc.vector.tensor_tensor(rest[:], whole, high, SUBTRACT)
-        nc.vector.tensor_tensor(low, rest[:], middle, SUBTRACT)
-        nc.vector.memset(zeros, 0.0)
-        ident = held.tile([P, P], BF16, name="ident")
-        make_identity(nc, ident[:])
-        cen_rows = held.tile([P, SETS, O], BF16, name="cen_rows")
-        for s in range(SETS):
-            turned = small.tile([P, O], BF16, name="turned")
-            for r in range(BLOCKS):
-                nc.tensor.transpose(
-                    turned[:, r * P : (r + 1) * P],
-                    split[:, r * SETS + s, :, :].rearrange("o piece f -> o (piece f)"),
-                    ident[:],
-                )
-            nc.vector.tensor_copy(cen_rows[:, s, :], turned[:])
-        pick_col = held.tile([P, FEATS], BF16, name="pick_col")
-        nc.vector.tensor_tensor(pick_col[:], ident[:, :FEATS], ident[:, FEATS : 2 * FEATS], ADD)
-        nc.vector.tensor_tensor(pick_col[:], pick_col[:], ident[:, 2 * FEATS : 3 * FEATS], ADD)
-
         ones_row = held.tile([1, N], F32, name="ones_row")
         nc.vector.memset(ones_row[:], 1.0)
         warm = held.tile([1, N], F32, name="warm")
         nc.scalar.activation(warm[:], ones_row[:], LN)
-        b_ps = small.tile([P, BLOCKS * N], F32, name="b_ps")
+        b_ps = spread.tile([P, BLOCKS * N], F32, name="b_ps")
         for r in range(BLOCKS):
             nc.tensor.matmul(
                 b_ps[:, r * N : (r + 1) * N],
@@ -91,46 +61,50 @@ def tile_fuzzybelllayer_kernel(tc, base, x, amat, cen, b, offs, out):
         b_wide = held.tile([P, BLOCKS * N], F32, name="b_wide")
         nc.vector.tensor_copy(b_wide[:], b_ps[:])
 
-        total = [held.tile([P, LANES, GROUP * N], F32, name=f"total{r}") for r in range(BLOCKS)]
-        for step in range(GROUPS + LAG * (BLOCKS - 1)):
-            for r in range(BLOCKS):
-                g = step - LAG * r
-                if g < 0 or g >= GROUPS:
-                    continue
-                first = g * GROUP
-                y = banks.tile([P, GROUP, N], F32, name="y")
+        for r in range(BLOCKS):
+            total = held.tile([P, LANES, GROUP * N], F32, name=f"total{r}")
+            for g in range(D // GROUP):
+                lane = total[:, g % LANES, :]
+                sq = lane if g < LANES else squares.tile([P, GROUP * N], F32, name="sq")[:]
+                z = products.tile([P, GROUP * N], F32, name="z")
                 for q in range(GROUP):
-                    i = first + q
+                    i = g * GROUP + q
                     nc.tensor.matmul(
-                        y[:, q, :],
+                        z[:, q * N : (q + 1) * N],
                         amat_sb[i // LOAD][:, i % LOAD, r * P : (r + 1) * P],
                         x_sb[:],
-                        start=(q == 0),
-                        stop=False,
+                        start=True,
+                        stop=True,
                     )
-                picked = pick_col[:, first % FEATS : first % FEATS + GROUP]
-                nc.tensor.matmul(
-                    y[:],
-                    cen_rows[:, first // FEATS, r * P : (r + 1) * P],
-                    picked.unsqueeze(2).to_broadcast([P, GROUP, N]),
-                    start=False,
-                    stop=True,
-                )
-                lane = total[r][:, g % LANES, :]
-                sq = lane if g < LANES else squares.tile([P, GROUP * N], F32, name="sq")[:]
-                nc.scalar.activation(sq, y[:].rearrange("o q j -> o (q j)"), SQUARE)
+                if g % RELIEF == RELIEF // 2:
+                    y = squares.tile([P, GROUP * N], F32, name="y")
+                    nc.vector.tensor_tensor(
+                        y[:].rearrange("o (q j) -> o q j", j=N),
+                        z[:].rearrange("o (q j) -> o q j", j=N),
+                        cen_sb[r][:, g * GROUP : (g + 1) * GROUP].unsqueeze(2).to_broadcast([P, GROUP, N]),
+                        ADD,
+                    )
+                    nc.vector.tensor_tensor(sq, y[:], y[:], MULT)
+                else:
+                    for q in range(GROUP):
+                        i = g * GROUP + q
+                        nc.scalar.activation(
+                            sq[:, q * N : (q + 1) * N],
+                            z[:, q * N : (q + 1) * N],
+                            SQUARE,
+                            bias=cen_sb[r][:, i : i + 1],
+                        )
                 if g >= LANES:
                     nc.vector.tensor_tensor(lane, lane, sq, ADD)
-                if g < GROUPS - 1:
-                    continue
 
-                r2 = held.tile([P, N], F32, name=f"r2_{r}")
-                nc.vector.tensor_reduce(
-                    r2[:], total[r][:].rearrange("o l (q j) -> o j (l q)", j=N), mybir.AxisListType.X, ADD
-                )
-                log_r2 = held.tile([P, N], F32, name=f"log_r2_{r}")
-                nc.scalar.activation(log_r2[:], r2[:], LN)
-                nc.vector.tensor_tensor(
-                    window[r][:].indirect(offsets[:]), log_r2[:], b_wide[:, r * N : (r + 1) * N], MULT
-                )
-                nc.sync.dma_start(out[r * P : (r + 1) * P, :], window[r][:])
+            r2 = held.tile([P, N], F32, name=f"r2_{r}")
+            nc.vector.tensor_reduce(
+                r2[:], total[:].rearrange("o l (q j) -> o j (l q)", j=N), mybir.AxisListType.X, ADD
+            )
+            log_r2 = held.tile([P, N], F32, name=f"log_r2_{r}")
+            nc.scalar.activation(log_r2[:], r2[:], LN)
+
+            nc.vector.tensor_tensor(
+                window[r][:].indirect(offsets[:]), log_r2[:], b_wide[:, r * N : (r + 1) * N], MULT
+            )
+            nc.sync.dma_start(out[r * P : (r + 1) * P, :], window[r][:])

@@ -14,7 +14,6 @@ BLOCKS = O // P
 LOAD = 8
 GROUP = 4
 LANES = 2
-RELIEF = 16
 
 FLOPS = 2 * D * D * O * N
 
@@ -76,24 +75,14 @@ def tile_fuzzybelllayer_kernel(tc, base, x, amat, cen, b, offs, out):
                         start=True,
                         stop=True,
                     )
-                if g % RELIEF == RELIEF // 2:
-                    y = squares.tile([P, GROUP * N], F32, name="y")
-                    nc.vector.tensor_tensor(
-                        y[:].rearrange("o (q j) -> o q j", j=N),
-                        z[:].rearrange("o (q j) -> o q j", j=N),
-                        cen_sb[r][:, g * GROUP : (g + 1) * GROUP].unsqueeze(2).to_broadcast([P, GROUP, N]),
-                        ADD,
+                for q in range(GROUP):
+                    i = g * GROUP + q
+                    nc.scalar.activation(
+                        sq[:, q * N : (q + 1) * N],
+                        z[:, q * N : (q + 1) * N],
+                        SQUARE,
+                        bias=cen_sb[r][:, i : i + 1],
                     )
-                    nc.vector.tensor_tensor(sq, y[:], y[:], MULT)
-                else:
-                    for q in range(GROUP):
-                        i = g * GROUP + q
-                        nc.scalar.activation(
-                            sq[:, q * N : (q + 1) * N],
-                            z[:, q * N : (q + 1) * N],
-                            SQUARE,
-                            bias=cen_sb[r][:, i : i + 1],
-                        )
                 if g >= LANES:
                     nc.vector.tensor_tensor(lane, lane, sq, ADD)
 

@@ -1,9 +1,11 @@
 import concourse.mybir as mybir
+from concourse.masks import make_identity
 
 F32 = mybir.dt.float32
 BF16 = mybir.dt.bfloat16
 U16 = mybir.dt.uint16
 ADD = mybir.AluOpType.add
+SUBTRACT = mybir.AluOpType.subtract
 MULT = mybir.AluOpType.mult
 SQUARE = mybir.ActivationFunctionType.Square
 LN = mybir.ActivationFunctionType.Ln
@@ -14,6 +16,9 @@ BLOCKS = O // P
 LOAD = 8
 GROUP = 4
 LANES = 2
+SLOTS = 4
+FEATS = P // SLOTS
+SETS = D // FEATS
 
 FLOPS = 2 * D * D * O * N
 
@@ -22,19 +27,18 @@ def tile_fuzzybelllayer_kernel(tc, base, x, amat, cen, b, offs, out):
     nc = tc.nc
     with (
         tc.tile_pool(name="held", bufs=1) as held,
-        tc.tile_pool(name="squares", bufs=4) as squares,
-        tc.psum_pool(name="spread", bufs=1) as spread,
-        tc.psum_pool(name="products", bufs=7) as products,
+        tc.tile_pool(name="squares", bufs=8) as squares,
+        tc.psum_pool(name="small", bufs=1) as small,
+        tc.psum_pool(name="banks", bufs=6) as banks,
     ):
         offsets = held.tile([P, N // 16], U16, name="offsets")
         nc.sync.dma_start(offsets[:], offs)
+        cen_sb = held.tile([P, BLOCKS, D], F32, name="cen_sb")
+        nc.sync.dma_start(cen_sb[:], cen.rearrange("(r o) i -> o r i", o=P))
         x_sb = held.tile([P, N], BF16, name="x_sb")
         nc.sync.dma_start(x_sb[:], x)
         b_row = held.tile([1, O], F32, name="b_row")
         nc.sync.dma_start(b_row[:], b.rearrange("o one -> one o"))
-        cen_sb = [held.tile([P, D], F32, name=f"cen{r}") for r in range(BLOCKS)]
-        for r in range(BLOCKS):
-            nc.sync.dma_start(cen_sb[r][:], cen[r * P : (r + 1) * P, :])
 
         amat_sb = [held.tile([P, LOAD, O], BF16, name=f"amat{c}") for c in range(D // LOAD)]
         for c in range(D // LOAD):
@@ -44,11 +48,36 @@ def tile_fuzzybelllayer_kernel(tc, base, x, amat, cen, b, offs, out):
         for r in range(BLOCKS):
             nc.scalar.dma_start(window[r][:], base[r * P : (r + 1) * P, :])
 
+        split = held.tile([P, BLOCKS * SETS, SLOTS, FEATS], BF16, name="split")
+        whole = cen_sb[:].rearrange("o r (s f) -> o (r s) f", f=FEATS)
+        high, middle, low, zeros = (split[:, :, slot, :] for slot in range(SLOTS))
+        rest = held.tile([P, BLOCKS * SETS, FEATS], F32, name="rest")
+        nc.vector.tensor_copy(high, whole)
+        nc.vector.tensor_tensor(middle, whole, high, SUBTRACT)
+        nc.vector.tensor_tensor(rest[:], whole, high, SUBTRACT)
+        nc.vector.tensor_tensor(low, rest[:], middle, SUBTRACT)
+        nc.vector.memset(zeros, 0.0)
+        ident = held.tile([P, P], BF16, name="ident")
+        make_identity(nc, ident[:])
+        cen_rows = held.tile([P, SETS, O], BF16, name="cen_rows")
+        for s in range(SETS):
+            turned = small.tile([P, O], BF16, name="turned")
+            for r in range(BLOCKS):
+                nc.tensor.transpose(
+                    turned[:, r * P : (r + 1) * P],
+                    split[:, r * SETS + s, :, :].rearrange("o piece f -> o (piece f)"),
+                    ident[:],
+                )
+            nc.vector.tensor_copy(cen_rows[:, s, :], turned[:])
+        pick_col = held.tile([P, FEATS], BF16, name="pick_col")
+        nc.vector.tensor_tensor(pick_col[:], ident[:, :FEATS], ident[:, FEATS : 2 * FEATS], ADD)
+        nc.vector.tensor_tensor(pick_col[:], pick_col[:], ident[:, 2 * FEATS : 3 * FEATS], ADD)
+
         ones_row = held.tile([1, N], F32, name="ones_row")
         nc.vector.memset(ones_row[:], 1.0)
         warm = held.tile([1, N], F32, name="warm")
         nc.scalar.activation(warm[:], ones_row[:], LN)
-        b_ps = spread.tile([P, BLOCKS * N], F32, name="b_ps")
+        b_ps = small.tile([P, BLOCKS * N], F32, name="b_ps")
         for r in range(BLOCKS):
             nc.tensor.matmul(
                 b_ps[:, r * N : (r + 1) * N],
@@ -63,26 +92,28 @@ def tile_fuzzybelllayer_kernel(tc, base, x, amat, cen, b, offs, out):
         for r in range(BLOCKS):
             total = held.tile([P, LANES, GROUP * N], F32, name=f"total{r}")
             for g in range(D // GROUP):
-                lane = total[:, g % LANES, :]
-                sq = lane if g < LANES else squares.tile([P, GROUP * N], F32, name="sq")[:]
-                z = products.tile([P, GROUP * N], F32, name="z")
+                first = g * GROUP
+                y = banks.tile([P, GROUP, N], F32, name="y")
                 for q in range(GROUP):
-                    i = g * GROUP + q
+                    i = first + q
                     nc.tensor.matmul(
-                        z[:, q * N : (q + 1) * N],
+                        y[:, q, :],
                         amat_sb[i // LOAD][:, i % LOAD, r * P : (r + 1) * P],
                         x_sb[:],
-                        start=True,
-                        stop=True,
+                        start=(q == 0),
+                        stop=False,
                     )
-                for q in range(GROUP):
-                    i = g * GROUP + q
-                    nc.scalar.activation(
-                        sq[:, q * N : (q + 1) * N],
-                        z[:, q * N : (q + 1) * N],
-                        SQUARE,
-                        bias=cen_sb[r][:, i : i + 1],
-                    )
+                picked = pick_col[:, first % FEATS : first % FEATS + GROUP]
+                nc.tensor.matmul(
+                    y[:],
+                    cen_rows[:, first // FEATS, r * P : (r + 1) * P],
+                    picked.unsqueeze(2).to_broadcast([P, GROUP, N]),
+                    start=False,
+                    stop=True,
+                )
+                lane = total[:, g % LANES, :]
+                sq = lane if g < LANES else squares.tile([P, GROUP * N], F32, name="sq")[:]
+                nc.scalar.activation(sq, y[:].rearrange("o q j -> o (q j)"), SQUARE)
                 if g >= LANES:
                     nc.vector.tensor_tensor(lane, lane, sq, ADD)
 

@@ -16,6 +16,7 @@ BLOCKS = O // P
 LOAD = 8
 GROUP = 4
 LANES = 2
+EARLY = 6
 SLOTS = 4
 FEATS = P // SLOTS
 SETS = D // FEATS
@@ -94,26 +95,36 @@ def tile_fuzzybelllayer_kernel(tc, base, x, amat, cen, b, offs, out):
             for g in range(D // GROUP):
                 first = g * GROUP
                 y = banks.tile([P, GROUP, N], F32, name="y")
+                early = r == 0 and g < EARLY
                 for q in range(GROUP):
                     i = first + q
                     nc.tensor.matmul(
                         y[:, q, :],
                         amat_sb[i // LOAD][:, i % LOAD, r * P : (r + 1) * P],
                         x_sb[:],
-                        start=(q == 0),
-                        stop=False,
+                        start=(q == 0 or early),
+                        stop=early,
                     )
-                picked = pick_col[:, first % FEATS : first % FEATS + GROUP]
-                nc.tensor.matmul(
-                    y[:],
-                    cen_rows[:, first // FEATS, r * P : (r + 1) * P],
-                    picked.unsqueeze(2).to_broadcast([P, GROUP, N]),
-                    start=False,
-                    stop=True,
-                )
                 lane = total[:, g % LANES, :]
                 sq = lane if g < LANES else squares.tile([P, GROUP * N], F32, name="sq")[:]
-                nc.scalar.activation(sq, y[:].rearrange("o q j -> o (q j)"), SQUARE)
+                if early:
+                    for q in range(GROUP):
+                        nc.scalar.activation(
+                            sq[:, q * N : (q + 1) * N],
+                            y[:, q, :],
+                            SQUARE,
+                            bias=cen_sb[:, r, first + q : first + q + 1],
+                        )
+                else:
+                    picked = pick_col[:, first % FEATS : first % FEATS + GROUP]
+                    nc.tensor.matmul(
+                        y[:],
+                        cen_rows[:, first // FEATS, r * P : (r + 1) * P],
+                        picked.unsqueeze(2).to_broadcast([P, GROUP, N]),
+                        start=False,
+                        stop=True,
+                    )
+                    nc.scalar.activation(sq, y[:].rearrange("o q j -> o (q j)"), SQUARE)
                 if g >= LANES:
                     nc.vector.tensor_tensor(lane, lane, sq, ADD)
 

@@ -15,7 +15,6 @@ O, D, S, N = 256, 128, 256, 128
 BLOCKS = O // P
 LOAD = 8
 GROUP = 4
-LANES = 2
 EARLY = 6
 SLOTS = 4
 FEATS = P // SLOTS
@@ -90,12 +89,12 @@ def tile_fuzzybelllayer_kernel(tc, base, x, amat, cen, b, offs, out):
         b_wide = held.tile([P, BLOCKS * N], F32, name="b_wide")
         nc.vector.tensor_copy(b_wide[:], b_ps[:])
 
-        for r in range(BLOCKS):
-            total = held.tile([P, LANES, GROUP * N], F32, name=f"total{r}")
-            for g in range(D // GROUP):
-                first = g * GROUP
+        total = [held.tile([P, GROUP * N], F32, name=f"total{r}") for r in range(BLOCKS)]
+        for g in range(D // GROUP):
+            first = g * GROUP
+            for r in range(BLOCKS):
                 y = banks.tile([P, GROUP, N], F32, name="y")
-                early = r == 0 and g < EARLY
+                early = g * BLOCKS + r < EARLY
                 for q in range(GROUP):
                     i = first + q
                     nc.tensor.matmul(
@@ -105,8 +104,7 @@ def tile_fuzzybelllayer_kernel(tc, base, x, amat, cen, b, offs, out):
                         start=(q == 0 or early),
                         stop=early,
                     )
-                lane = total[:, g % LANES, :]
-                sq = lane if g < LANES else squares.tile([P, GROUP * N], F32, name="sq")[:]
+                sq = total[r][:] if g == 0 else squares.tile([P, GROUP * N], F32, name="sq")[:]
                 if early:
                     for q in range(GROUP):
                         nc.scalar.activation(
@@ -125,17 +123,19 @@ def tile_fuzzybelllayer_kernel(tc, base, x, amat, cen, b, offs, out):
                         stop=True,
                     )
                     nc.scalar.activation(sq, y[:].rearrange("o q j -> o (q j)"), SQUARE)
-                if g >= LANES:
-                    nc.vector.tensor_tensor(lane, lane, sq, ADD)
+                if g > 0:
+                    nc.vector.tensor_tensor(total[r][:], total[r][:], sq, ADD)
 
-            r2 = held.tile([P, N], F32, name=f"r2_{r}")
-            nc.vector.tensor_reduce(
-                r2[:], total[:].rearrange("o l (q j) -> o j (l q)", j=N), mybir.AxisListType.X, ADD
-            )
-            log_r2 = held.tile([P, N], F32, name=f"log_r2_{r}")
-            nc.scalar.activation(log_r2[:], r2[:], LN)
-
+        half = [held.tile([P, 2 * N], F32, name=f"half{r}") for r in range(BLOCKS)]
+        r2 = [held.tile([P, N], F32, name=f"r2_{r}") for r in range(BLOCKS)]
+        log_r2 = [held.tile([P, N], F32, name=f"log_r2_{r}") for r in range(BLOCKS)]
+        for r in range(BLOCKS):
+            nc.vector.tensor_tensor(half[r][:], total[r][:, : 2 * N], total[r][:, 2 * N :], ADD)
+        for r in range(BLOCKS):
+            nc.vector.tensor_tensor(r2[r][:], half[r][:, :N], half[r][:, N:], ADD)
+            nc.scalar.activation(log_r2[r][:], r2[r][:], LN)
+        for r in range(BLOCKS):
             nc.vector.tensor_tensor(
-                window[r][:].indirect(offsets[:]), log_r2[:], b_wide[:, r * N : (r + 1) * N], MULT
+                window[r][:].indirect(offsets[:]), log_r2[r][:], b_wide[:, r * N : (r + 1) * N], MULT
             )
             nc.sync.dma_start(out[r * P : (r + 1) * P, :], window[r][:])

@@ -15,7 +15,7 @@ O, D, S, N = 256, 128, 256, 128
 BLOCKS = O // P
 LOAD = 8
 GROUP = 4
-EARLY = 6
+EARLY = 8
 SLOTS = 4
 FEATS = P // SLOTS
 SETS = D // FEATS

@@ -31,22 +31,25 @@ def tile_fuzzybelllayer_kernel(tc, base, x, amat, cen, b, offs, out):
         tc.psum_pool(name="small", bufs=1) as small,
         tc.psum_pool(name="banks", bufs=6) as banks,
     ):
-        offsets = held.tile([P, N // 16], U16, name="offsets")
-        nc.sync.dma_start(offsets[:], offs)
-        cen_sb = held.tile([P, BLOCKS, D], F32, name="cen_sb")
-        nc.sync.dma_start(cen_sb[:], cen.rearrange("(r o) i -> o r i", o=P))
         x_sb = held.tile([P, N], BF16, name="x_sb")
         nc.sync.dma_start(x_sb[:], x)
+        amat_sb = [held.tile([P, LOAD, O], BF16, name=f"amat{c}") for c in range(D // LOAD)]
+        nc.sync.dma_start(amat_sb[0][:, :GROUP, :], amat[:, :GROUP, :])
+        cen_sb = held.tile([P, BLOCKS, D], F32, name="cen_sb")
+        nc.sync.dma_start(cen_sb[:], cen.rearrange("(r o) i -> o r i", o=P))
+        nc.sync.dma_start(amat_sb[0][:, GROUP:, :], amat[:, GROUP:LOAD, :])
+
+        offsets = held.tile([P, N // 16], U16, name="offsets")
+        nc.sync.dma_start(offsets[:], offs)
         b_row = held.tile([1, O], F32, name="b_row")
         nc.sync.dma_start(b_row[:], b.rearrange("o one -> one o"))
 
-        amat_sb = [held.tile([P, LOAD, O], BF16, name=f"amat{c}") for c in range(D // LOAD)]
-        for c in range(D // LOAD):
+        for c in range(1, D // LOAD):
             nc.sync.dma_start(amat_sb[c][:], amat[:, c * LOAD : (c + 1) * LOAD, :])
 
         window = [held.tile([P, S], F32, name=f"window{r}") for r in range(BLOCKS)]
         for r in range(BLOCKS):
-            nc.scalar.dma_start(window[r][:], base[r * P : (r + 1) * P, :])
+            nc.sync.dma_start(window[r][:], base[r * P : (r + 1) * P, :])
 
         split = held.tile([P, BLOCKS * SETS, SLOTS, FEATS], BF16, name="split")
         whole = cen_sb[:].rearrange("o r (s f) -> o (r s) f", f=FEATS)

@@ -9,11 +9,13 @@ SUBTRACT = mybir.AluOpType.subtract
 MULT = mybir.AluOpType.mult
 SQUARE = mybir.ActivationFunctionType.Square
 LN = mybir.ActivationFunctionType.Ln
+IDENTITY = mybir.ActivationFunctionType.Identity
 
 P = 128
 O, D, S, N = 256, 128, 256, 128
 BLOCKS = O // P
 LOAD = 8
+FIRST_PIECES = ((0, 2), (2, 4), (4, 8))
 GROUP = 4
 EARLY = 8
 SLOTS = 4
@@ -31,18 +33,18 @@ def tile_fuzzybelllayer_kernel(tc, base, x, amat, cen, b, offs, out):
         tc.psum_pool(name="small", bufs=1) as small,
         tc.psum_pool(name="banks", bufs=6) as banks,
     ):
+        cen_sb = held.tile([P, BLOCKS, D], F32, name="cen_sb")
+        nc.sync.dma_start(cen_sb[:], cen.rearrange("(r o) i -> o r i", o=P))
         x_sb = held.tile([P, N], BF16, name="x_sb")
         nc.sync.dma_start(x_sb[:], x)
         amat_sb = [held.tile([P, LOAD, O], BF16, name=f"amat{c}") for c in range(D // LOAD)]
-        nc.sync.dma_start(amat_sb[0][:, :GROUP, :], amat[:, :GROUP, :])
-        cen_sb = held.tile([P, BLOCKS, D], F32, name="cen_sb")
-        nc.sync.dma_start(cen_sb[:], cen.rearrange("(r o) i -> o r i", o=P))
-        nc.sync.dma_start(amat_sb[0][:, GROUP:, :], amat[:, GROUP:LOAD, :])
+        for lo, hi in FIRST_PIECES:
+            nc.sync.dma_start(amat_sb[0][:, lo:hi, :], amat[:, lo:hi, :])
 
         offsets = held.tile([P, N // 16], U16, name="offsets")
         nc.sync.dma_start(offsets[:], offs)
-        b_row = held.tile([1, O], F32, name="b_row")
-        nc.sync.dma_start(b_row[:], b.rearrange("o one -> one o"))
+        b_col = held.tile([P, BLOCKS], F32, name="b_col")
+        nc.sync.dma_start(b_col[:], b.rearrange("(r o) one -> o (r one)", o=P))
 
         for c in range(1, D // LOAD):
             nc.sync.dma_start(amat_sb[c][:], amat[:, c * LOAD : (c + 1) * LOAD, :])
@@ -76,21 +78,10 @@ def tile_fuzzybelllayer_kernel(tc, base, x, amat, cen, b, offs, out):
         nc.vector.tensor_tensor(pick_col[:], ident[:, :FEATS], ident[:, FEATS : 2 * FEATS], ADD)
         nc.vector.tensor_tensor(pick_col[:], pick_col[:], ident[:, 2 * FEATS : 3 * FEATS], ADD)
 
-        ones_row = held.tile([1, N], F32, name="ones_row")
-        nc.vector.memset(ones_row[:], 1.0)
-        warm = held.tile([1, N], F32, name="warm")
-        nc.scalar.activation(warm[:], ones_row[:], LN)
-        b_ps = small.tile([P, BLOCKS * N], F32, name="b_ps")
-        for r in range(BLOCKS):
-            nc.tensor.matmul(
-                b_ps[:, r * N : (r + 1) * N],
-                b_row[:, r * P : (r + 1) * P],
-                ones_row[:],
-                start=True,
-                stop=True,
-            )
-        b_wide = held.tile([P, BLOCKS * N], F32, name="b_wide")
-        nc.vector.tensor_copy(b_wide[:], b_ps[:])
+        ones = held.tile([P, N], F32, name="ones")
+        nc.vector.memset(ones[:], 1.0)
+        warm = held.tile([P, N], F32, name="warm")
+        nc.scalar.activation(warm[:], ones[:], LN)
 
         total = [held.tile([P, GROUP * N], F32, name=f"total{r}") for r in range(BLOCKS)]
         for g in range(D // GROUP):
@@ -128,6 +119,10 @@ def tile_fuzzybelllayer_kernel(tc, base, x, amat, cen, b, offs, out):
                     nc.scalar.activation(sq, y[:].rearrange("o q j -> o (q j)"), SQUARE)
                 if g > 0:
                     nc.vector.tensor_tensor(total[r][:], total[r][:], sq, ADD)
+
+        b_wide = held.tile([P, BLOCKS * N], F32, name="b_wide")
+        for r in range(BLOCKS):
+            nc.scalar.activation(b_wide[:, r * N : (r + 1) * N], ones[:], IDENTITY, scale=b_col[:, r : r + 1])
 
         half = [held.tile([P, 2 * N], F32, name=f"half{r}") for r in range(BLOCKS)]
         r2 = [held.tile([P, N], F32, name=f"r2_{r}") for r in range(BLOCKS)]

@@ -17,7 +17,7 @@ BLOCKS = O // P
 LOAD = 8
 FIRST_PIECES = ((0, 2), (2, 4), (4, 8))
 GROUP = 4
-EARLY = 8
+EARLY = 12
 SLOTS = 4
 FEATS = P // SLOTS
 SETS = D // FEATS

@@ -17,6 +17,7 @@ BLOCKS = O // P
 LOAD = 8
 FIRST_PIECES = ((0, 2), (2, 4), (4, 8))
 GROUP = 4
+TURN_AT = 2
 EARLY = 12
 SLOTS = 4
 FEATS = P // SLOTS
@@ -30,7 +31,7 @@ def tile_fuzzybelllayer_kernel(tc, base, x, amat, cen, b, offs, out):
     with (
         tc.tile_pool(name="held", bufs=1) as held,
         tc.tile_pool(name="squares", bufs=8) as squares,
-        tc.psum_pool(name="small", bufs=1) as small,
+        tc.psum_pool(name="small", bufs=2) as small,
         tc.psum_pool(name="banks", bufs=6) as banks,
     ):
         cen_sb = held.tile([P, BLOCKS, D], F32, name="cen_sb")
@@ -65,15 +66,18 @@ def tile_fuzzybelllayer_kernel(tc, base, x, amat, cen, b, offs, out):
         ident = held.tile([P, P], BF16, name="ident")
         make_identity(nc, ident[:])
         cen_rows = held.tile([P, SETS, O], BF16, name="cen_rows")
-        for s in range(SETS):
-            turned = small.tile([P, O], BF16, name="turned")
-            for r in range(BLOCKS):
-                nc.tensor.transpose(
-                    turned[:, r * P : (r + 1) * P],
-                    split[:, r * SETS + s, :, :].rearrange("o piece f -> o (piece f)"),
-                    ident[:],
-                )
-            nc.vector.tensor_copy(cen_rows[:, s, :], turned[:])
+
+        def turn_pieces():
+            for s in range(SETS):
+                turned = small.tile([P, O], BF16, name="turned")
+                for r in range(BLOCKS):
+                    nc.tensor.transpose(
+                        turned[:, r * P : (r + 1) * P],
+                        split[:, r * SETS + s, :, :].rearrange("o piece f -> o (piece f)"),
+                        ident[:],
+                    )
+                nc.vector.tensor_copy(cen_rows[:, s, :], turned[:])
+
         pick_col = held.tile([P, FEATS], BF16, name="pick_col")
         nc.vector.tensor_tensor(pick_col[:], ident[:, :FEATS], ident[:, FEATS : 2 * FEATS], ADD)
         nc.vector.tensor_tensor(pick_col[:], pick_col[:], ident[:, 2 * FEATS : 3 * FEATS], ADD)
@@ -86,6 +90,8 @@ def tile_fuzzybelllayer_kernel(tc, base, x, amat, cen, b, offs, out):
         total = [held.tile([P, GROUP * N], F32, name=f"total{r}") for r in range(BLOCKS)]
         for g in range(D // GROUP):
             first = g * GROUP
+            if g == TURN_AT:
+                turn_pieces()
             for r in range(BLOCKS):
                 y = banks.tile([P, GROUP, N], F32, name="y")
                 early = g * BLOCKS + r < EARLY

@@ -15,7 +15,6 @@ P = 128
 O, D, S, N = 256, 128, 256, 128
 BLOCKS = O // P
 LOAD = 8
-FIRST_PIECES = ((0, 2), (2, 4), (4, 8))
 GROUP = 4
 TURN_AT = 2
 EARLY = 12
@@ -31,16 +30,17 @@ def tile_fuzzybelllayer_kernel(tc, base, x, amat, cen, b, offs, out):
     with (
         tc.tile_pool(name="held", bufs=1) as held,
         tc.tile_pool(name="squares", bufs=8) as squares,
-        tc.psum_pool(name="small", bufs=2) as small,
-        tc.psum_pool(name="banks", bufs=6) as banks,
+        tc.psum_pool(name="small", bufs=1) as small,
+        tc.psum_pool(name="banks", bufs=7) as banks,
     ):
-        cen_sb = held.tile([P, BLOCKS, D], F32, name="cen_sb")
-        nc.sync.dma_start(cen_sb[:], cen.rearrange("(r o) i -> o r i", o=P))
         x_sb = held.tile([P, N], BF16, name="x_sb")
         nc.sync.dma_start(x_sb[:], x)
         amat_sb = [held.tile([P, LOAD, O], BF16, name=f"amat{c}") for c in range(D // LOAD)]
-        for lo, hi in FIRST_PIECES:
-            nc.sync.dma_start(amat_sb[0][:, lo:hi, :], amat[:, lo:hi, :])
+        nc.sync.dma_start(amat_sb[0][:, :GROUP, :P], amat[:, :GROUP, :P])
+        cen_sb = held.tile([P, BLOCKS, D], F32, name="cen_sb")
+        nc.sync.dma_start(cen_sb[:], cen.rearrange("(r o) i -> o r i", o=P))
+        nc.sync.dma_start(amat_sb[0][:, :GROUP, P:], amat[:, :GROUP, P:])
+        nc.sync.dma_start(amat_sb[0][:, GROUP:, :], amat[:, GROUP:LOAD, :])
 
         offsets = held.tile([P, N // 16], U16, name="offsets")
         nc.sync.dma_start(offsets[:], offs)
@@ -68,15 +68,15 @@ def tile_fuzzybelllayer_kernel(tc, base, x, amat, cen, b, offs, out):
         cen_rows = held.tile([P, SETS, O], BF16, name="cen_rows")
 
         def turn_pieces():
+            turned = small.tile([P, SETS, O], BF16, name="turned")
             for s in range(SETS):
-                turned = small.tile([P, O], BF16, name="turned")
                 for r in range(BLOCKS):
                     nc.tensor.transpose(
-                        turned[:, r * P : (r + 1) * P],
+                        turned[:, s, r * P : (r + 1) * P],
                         split[:, r * SETS + s, :, :].rearrange("o piece f -> o (piece f)"),
                         ident[:],
                     )
-                nc.vector.tensor_copy(cen_rows[:, s, :], turned[:])
+            nc.vector.tensor_copy(cen_rows[:], turned[:])
 
         pick_col = held.tile([P, FEATS], BF16, name="pick_col")
         nc.vector.tensor_tensor(pick_col[:], ident[:, :FEATS], ident[:, FEATS : 2 * FEATS], ADD)

import concourse.mybir as mybir
from concourse.masks import make_identity

F32 = mybir.dt.float32
BF16 = mybir.dt.bfloat16
U16 = mybir.dt.uint16
ADD = mybir.AluOpType.add
SUBTRACT = mybir.AluOpType.subtract
MULT = mybir.AluOpType.mult
SQUARE = mybir.ActivationFunctionType.Square
LN = mybir.ActivationFunctionType.Ln
IDENTITY = mybir.ActivationFunctionType.Identity

P = 128
O, D, S, N = 256, 128, 256, 128
BLOCKS = O // P
LOAD = 8
GROUP = 4
TURN_AT = 2
EARLY = 12
SLOTS = 4
FEATS = P // SLOTS
SETS = D // FEATS

FLOPS = 2 * D * D * O * N


def tile_fuzzybelllayer_kernel(tc, base, x, amat, cen, b, offs, out):
    nc = tc.nc
    with (
        tc.tile_pool(name="held", bufs=1) as held,
        tc.tile_pool(name="squares", bufs=8) as squares,
        tc.psum_pool(name="small", bufs=1) as small,
        tc.psum_pool(name="banks", bufs=7) as banks,
    ):
        x_sb = held.tile([P, N], BF16, name="x_sb")
        nc.sync.dma_start(x_sb[:], x)
        amat_sb = [held.tile([P, LOAD, O], BF16, name=f"amat{c}") for c in range(D // LOAD)]
        nc.sync.dma_start(amat_sb[0][:, :GROUP, :P], amat[:, :GROUP, :P])
        cen_sb = held.tile([P, BLOCKS, D], F32, name="cen_sb")
        nc.sync.dma_start(cen_sb[:], cen.rearrange("(r o) i -> o r i", o=P))
        nc.sync.dma_start(amat_sb[0][:, :GROUP, P:], amat[:, :GROUP, P:])
        nc.sync.dma_start(amat_sb[0][:, GROUP:, :], amat[:, GROUP:LOAD, :])

        offsets = held.tile([P, N // 16], U16, name="offsets")
        nc.sync.dma_start(offsets[:], offs)
        b_col = held.tile([P, BLOCKS], F32, name="b_col")
        nc.sync.dma_start(b_col[:], b.rearrange("(r o) one -> o (r one)", o=P))

        for c in range(1, D // LOAD):
            nc.sync.dma_start(amat_sb[c][:], amat[:, c * LOAD : (c + 1) * LOAD, :])

        window = [held.tile([P, S], F32, name=f"window{r}") for r in range(BLOCKS)]
        for r in range(BLOCKS):
            nc.sync.dma_start(window[r][:], base[r * P : (r + 1) * P, :])

        split = held.tile([P, BLOCKS * SETS, SLOTS, FEATS], BF16, name="split")
        whole = cen_sb[:].rearrange("o r (s f) -> o (r s) f", f=FEATS)
        high, middle, low, zeros = (split[:, :, slot, :] for slot in range(SLOTS))
        rest = held.tile([P, BLOCKS * SETS, FEATS], F32, name="rest")
        nc.vector.tensor_copy(high, whole)
        nc.vector.tensor_tensor(middle, whole, high, SUBTRACT)
        nc.vector.tensor_tensor(rest[:], whole, high, SUBTRACT)
        nc.vector.tensor_tensor(low, rest[:], middle, SUBTRACT)
        nc.vector.memset(zeros, 0.0)
        ident = held.tile([P, P], BF16, name="ident")
        make_identity(nc, ident[:])
        cen_rows = held.tile([P, SETS, O], BF16, name="cen_rows")

        def turn_pieces():
            turned = small.tile([P, SETS, O], BF16, name="turned")
            for s in range(SETS):
                for r in range(BLOCKS):
                    nc.tensor.transpose(
                        turned[:, s, r * P : (r + 1) * P],
                        split[:, r * SETS + s, :, :].rearrange("o piece f -> o (piece f)"),
                        ident[:],
                    )
            nc.vector.tensor_copy(cen_rows[:], turned[:])

        pick_col = held.tile([P, FEATS], BF16, name="pick_col")
        nc.vector.tensor_tensor(pick_col[:], ident[:, :FEATS], ident[:, FEATS : 2 * FEATS], ADD)
        nc.vector.tensor_tensor(pick_col[:], pick_col[:], ident[:, 2 * FEATS : 3 * FEATS], ADD)

        ones = held.tile([P, N], F32, name="ones")
        nc.vector.memset(ones[:], 1.0)
        warm = held.tile([P, N], F32, name="warm")
        nc.scalar.activation(warm[:], ones[:], LN)

        total = [held.tile([P, GROUP * N], F32, name=f"total{r}") for r in range(BLOCKS)]
        for g in range(D // GROUP):
            first = g * GROUP
            if g == TURN_AT:
                turn_pieces()
            for r in range(BLOCKS):
                y = banks.tile([P, GROUP, N], F32, name="y")
                early = g * BLOCKS + r < EARLY
                for q in range(GROUP):
                    i = first + q
                    nc.tensor.matmul(
                        y[:, q, :],
                        amat_sb[i // LOAD][:, i % LOAD, r * P : (r + 1) * P],
                        x_sb[:],
                        start=(q == 0 or early),
                        stop=early,
                    )
                sq = total[r][:] if g == 0 else squares.tile([P, GROUP * N], F32, name="sq")[:]
                if early:
                    for q in range(GROUP):
                        nc.scalar.activation(
                            sq[:, q * N : (q + 1) * N],
                            y[:, q, :],
                            SQUARE,
                            bias=cen_sb[:, r, first + q : first + q + 1],
                        )
                else:
                    picked = pick_col[:, first % FEATS : first % FEATS + GROUP]
                    nc.tensor.matmul(
                        y[:],
                        cen_rows[:, first // FEATS, r * P : (r + 1) * P],
                        picked.unsqueeze(2).to_broadcast([P, GROUP, N]),
                        start=False,
                        stop=True,
                    )
                    nc.scalar.activation(sq, y[:].rearrange("o q j -> o (q j)"), SQUARE)
                if g > 0:
                    nc.vector.tensor_tensor(total[r][:], total[r][:], sq, ADD)

        b_wide = held.tile([P, BLOCKS * N], F32, name="b_wide")
        for r in range(BLOCKS):
            nc.scalar.activation(b_wide[:, r * N : (r + 1) * N], ones[:], IDENTITY, scale=b_col[:, r : r + 1])

        half = [held.tile([P, 2 * N], F32, name=f"half{r}") for r in range(BLOCKS)]
        r2 = [held.tile([P, N], F32, name=f"r2_{r}") for r in range(BLOCKS)]
        log_r2 = [held.tile([P, N], F32, name=f"log_r2_{r}") for r in range(BLOCKS)]
        for r in range(BLOCKS):
            nc.vector.tensor_tensor(half[r][:], total[r][:, : 2 * N], total[r][:, 2 * N :], ADD)
        for r in range(BLOCKS):
            nc.vector.tensor_tensor(r2[r][:], half[r][:, :N], half[r][:, N:], ADD)
            nc.scalar.activation(log_r2[r][:], r2[r][:], LN)
        for r in range(BLOCKS):
            nc.vector.tensor_tensor(
                window[r][:].indirect(offsets[:]), log_r2[r][:], b_wide[:, r * N : (r + 1) * N], MULT
            )
            nc.sync.dma_start(out[r * P : (r + 1) * P, :], window[r][:])
